import numpy as np
import ml_dtypes

BF16 = ml_dtypes.bfloat16


def bf(x):
    return np.asarray(x, np.float32).astype(BF16)


def f32(x):
    return np.asarray(x, np.float32)


def f64(x):
    return np.asarray(x).astype(np.float64)


def striped(idx):
    return np.tile(idx.reshape(-1, 16).T, (8, 1))


S, E, H, N, P, HH, GH = 2048, 128, 128, 256, 128, 256, 384


def setup_inputs():
    return {
        "table": bf(np.random.standard_normal((S, E))),
        "w_u": bf(np.random.standard_normal((E, H)) / np.sqrt(E)),
        "b_u": f32(0.2 * np.random.standard_normal((H, 1))),
        "u_bin": bf(np.random.standard_normal((HH, GH)) / np.sqrt(HH)),
        "b_bin": f32(0.2 * np.random.standard_normal((GH, 1))),
        "u_un": bf(np.random.standard_normal((H, GH)) / np.sqrt(H)),
        "b_un": f32(0.2 * np.random.standard_normal((GH, 1))),
        "offs": striped(np.random.permutation(np.tile(np.arange(S), 2))[:N]),
    }


def reference(table, w_u, b_u, u_bin, b_bin, u_un, b_un, offs):
    idx = offs[:16].T.reshape(-1)
    h = np.tanh(f64(w_u).T @ f64(table)[idx].T + f64(b_u))
    h_l, h_r = h[:, :P], h[:, P:]
    ub = f64(u_bin)[:H].T @ h_l + f64(u_bin)[H:].T @ h_r + f64(b_bin)
    uu = f64(u_un).T @ h_l + f64(b_un)
    return np.concatenate([ub, uu], axis=0)

@@ -1,0 +1,89 @@
+import concourse.mybir as mybir
+from concourse.masks import make_identity
+
+BF16, F32, U16 = mybir.dt.bfloat16, mybir.dt.float32, mybir.dt.uint16
+TANH = mybir.ActivationFunctionType.Tanh
+ADD = mybir.AluOpType.add
+
+P = 128
+WORDS = 2048
+LEAVES = 256
+GATES = 3
+CHUNKS = 4
+BLOCKS = WORDS // P // CHUNKS
+
+FLOPS = 2 * P * P * LEAVES + 2 * (2 * P) * (GATES * P) * P + 2 * P * (GATES * P) * P
+
+
+def tile_mixedaritytreelstm_kernel(tc, table, w_u, b_u, u_bin, b_bin, u_un, b_un, offs, out):
+    nc = tc.nc
+    with (
+        tc.tile_pool(name="held", bufs=1) as held,
+        tc.psum_pool(name="flip", bufs=2) as flip,
+        tc.psum_pool(name="psum", bufs=1) as psum,
+    ):
+        table_pieces = table.rearrange("(c b p) d -> c p b d", c=CHUNKS, p=P)
+        rows = [held.tile([P, BLOCKS, P], BF16, name=f"rows{c}") for c in range(CHUNKS)]
+        for c in range(CHUNKS):
+            queue = nc.sync if c % 2 == 0 else nc.scalar
+            queue.dma_start(rows[c][:], table_pieces[c])
+
+        offsets = held.tile([P, LEAVES // 16], U16, name="offsets")
+        nc.sync.dma_start(offsets[:], offs)
+
+        w_u_sb = held.tile([P, P], BF16, name="w_u_sb")
+        nc.sync.dma_start(w_u_sb[:], w_u)
+        u_bin_sb = held.tile([P, 2, GATES * P], BF16, name="u_bin_sb")
+        nc.scalar.dma_start(u_bin_sb[:], u_bin.rearrange("(c k) m -> k c m", k=P))
+        u_un_sb = held.tile([P, GATES * P], BF16, name="u_un_sb")
+        nc.scalar.dma_start(u_un_sb[:], u_un)
+
+        b_u_sb = held.tile([P, 1], F32, name="b_u_sb")
+        b_bin_sb = held.tile([P, GATES], F32, name="b_bin_sb")
+        b_un_sb = held.tile([P, GATES], F32, name="b_un_sb")
+        with nc.allow_non_contiguous_dma(reason="a bias lands one float32 to a partition"):
+            nc.sync.dma_start(b_u_sb[:], b_u)
+            nc.sync.dma_start(b_bin_sb[:], b_bin.rearrange("(g p) o -> p (g o)", p=P))
+            nc.sync.dma_start(b_un_sb[:], b_un.rearrange("(g p) o -> p (g o)", p=P))
+
+        identity = held.tile([P, P], BF16, name="identity")
+        make_identity(nc, identity[:])
+
+        scratch = held.tile([P, 1], F32, name="scratch")
+        nc.vector.memset(scratch[:], 0.0)
+        nc.scalar.activation(scratch[:], scratch[:], TANH)
+
+        table_t = held.tile([P, WORDS], BF16, name="table_t")
+        for c in range(CHUNKS):
+            flipped = flip.tile([P, BLOCKS, P], BF16, name="flipped")
+            for b in range(BLOCKS):
+                nc.tensor.transpose(flipped[:, b, :], rows[c][:, b, :], identity[:])
+            columns = table_t[:, c * BLOCKS * P : (c + 1) * BLOCKS * P]
+            if c % 2 == 0:
+                nc.vector.tensor_copy(columns, flipped[:].rearrange("d b p -> d (b p)"))
+            else:
+                nc.scalar.copy(columns, flipped[:].rearrange("d b p -> d (b p)"))
+
+        h_ps = psum.tile([P, LEAVES], F32, name="h_ps")
+        nc.tensor.matmul(h_ps[:], w_u_sb[:], table_t[:].indirect(offsets[:]), start=True, stop=True)
+        h = held.tile([P, LEAVES], BF16, name="h")
+        nc.scalar.activation(h[:], h_ps[:], TANH, bias=b_u_sb[:])
+        h_left, h_right = h[:, 0:P], h[:, P:LEAVES]
+
+        un_ps = psum.tile([P, GATES, P], F32, name="un_ps")
+        bin_ps = psum.tile([P, GATES, P], F32, name="bin_ps")
+        for g in range(GATES):
+            gate = slice(g * P, (g + 1) * P)
+            nc.tensor.matmul(un_ps[:, g, :], u_un_sb[:, gate], h_left, start=True, stop=True)
+        for g in range(GATES):
+            gate = slice(g * P, (g + 1) * P)
+            nc.tensor.matmul(bin_ps[:, g, :], u_bin_sb[:, 0, gate], h_left, start=True, stop=False)
+            nc.tensor.matmul(bin_ps[:, g, :], u_bin_sb[:, 1, gate], h_right, start=False, stop=True)
+
+        out_blocks = out.rearrange("(c g p) q -> c p g q", c=2, p=P)
+        un_sb = held.tile([P, GATES, P], F32, name="un_sb")
+        nc.vector.tensor_tensor(un_sb[:], un_ps[:], b_un_sb[:].unsqueeze(2).to_broadcast([P, GATES, P]), ADD)
+        nc.sync.dma_start(out_blocks[1], un_sb[:])
+        bin_sb = held.tile([P, GATES, P], F32, name="bin_sb")
+        nc.vector.tensor_tensor(bin_sb[:], bin_ps[:], b_bin_sb[:].unsqueeze(2).to_broadcast([P, GATES, P]), ADD)
+        nc.sync.dma_start(out_blocks[0], bin_sb[:])

@@ -3,87 +3,107 @@ from concourse.masks import make_identity
 
 BF16, F32, U16 = mybir.dt.bfloat16, mybir.dt.float32, mybir.dt.uint16
 TANH = mybir.ActivationFunctionType.Tanh
-ADD = mybir.AluOpType.add
+IDENTITY = mybir.ActivationFunctionType.Identity
 
 P = 128
 WORDS = 2048
 LEAVES = 256
-GATES = 3
+ROWS = 3
+BANK = 512
 CHUNKS = 4
-BLOCKS = WORDS // P // CHUNKS
+CHUNK = WORDS // CHUNKS
+RUN = CHUNK // P
+WARM_UPS = 3
 
-FLOPS = 2 * P * P * LEAVES + 2 * (2 * P) * (GATES * P) * P + 2 * P * (GATES * P) * P
+FLOPS = 2 * P * P * LEAVES + 2 * (2 * P) * (ROWS * P) * P + 2 * P * (ROWS * P) * P
 
 
 def tile_mixedaritytreelstm_kernel(tc, table, w_u, b_u, u_bin, b_bin, u_un, b_un, offs, out):
     nc = tc.nc
     with (
         tc.tile_pool(name="held", bufs=1) as held,
-        tc.psum_pool(name="flip", bufs=2) as flip,
         tc.psum_pool(name="psum", bufs=1) as psum,
     ):
-        table_pieces = table.rearrange("(c b p) d -> c p b d", c=CHUNKS, p=P)
-        rows = [held.tile([P, BLOCKS, P], BF16, name=f"rows{c}") for c in range(CHUNKS)]
+        rows = []
         for c in range(CHUNKS):
-            queue = nc.sync if c % 2 == 0 else nc.scalar
-            queue.dma_start(rows[c][:], table_pieces[c])
+            rows.append(held.tile([P, RUN, P], BF16, name=f"rows{c}"))
+            nc.sync.dma_start(rows[c][:], table[c * CHUNK : (c + 1) * CHUNK, :].rearrange("(p a) d -> p a d", a=RUN))
 
         offsets = held.tile([P, LEAVES // 16], U16, name="offsets")
         nc.sync.dma_start(offsets[:], offs)
 
         w_u_sb = held.tile([P, P], BF16, name="w_u_sb")
         nc.sync.dma_start(w_u_sb[:], w_u)
-        u_bin_sb = held.tile([P, 2, GATES * P], BF16, name="u_bin_sb")
-        nc.scalar.dma_start(u_bin_sb[:], u_bin.rearrange("(c k) m -> k c m", k=P))
-        u_un_sb = held.tile([P, GATES * P], BF16, name="u_un_sb")
-        nc.scalar.dma_start(u_un_sb[:], u_un)
 
         b_u_sb = held.tile([P, 1], F32, name="b_u_sb")
-        b_bin_sb = held.tile([P, GATES], F32, name="b_bin_sb")
-        b_un_sb = held.tile([P, GATES], F32, name="b_un_sb")
-        with nc.allow_non_contiguous_dma(reason="a bias lands one float32 to a partition"):
-            nc.sync.dma_start(b_u_sb[:], b_u)
-            nc.sync.dma_start(b_bin_sb[:], b_bin.rearrange("(g p) o -> p (g o)", p=P))
-            nc.sync.dma_start(b_un_sb[:], b_un.rearrange("(g p) o -> p (g o)", p=P))
+        nc.sync.dma_start(b_u_sb[:], b_u)
+        u_un_sb = held.tile([P, ROWS * P], BF16, name="u_un_sb")
+        nc.sync.dma_start(u_un_sb[:], u_un)
+        u_bin_sb = held.tile([P, 2, ROWS * P], BF16, name="u_bin_sb")
+        nc.sync.dma_start(u_bin_sb[:], u_bin.rearrange("(c k) m -> k c m", k=P))
+        b_un_sb = held.tile([P, ROWS], F32, name="b_un_sb")
+        nc.sync.dma_start(b_un_sb[:], b_un.rearrange("(p r) o -> p (r o)", r=ROWS))
+        b_bin_sb = held.tile([P, ROWS], F32, name="b_bin_sb")
+        nc.sync.dma_start(b_bin_sb[:], b_bin.rearrange("(p r) o -> p (r o)", r=ROWS))
+
+        u_un_thirds = u_un_sb[:].rearrange("k (p r) -> k r p", r=ROWS)
+        u_bin_thirds = u_bin_sb[:].rearrange("k c (p r) -> k c r p", r=ROWS)
+
+        scratch = held.tile([P, 1], F32, name="scratch")
+        nc.gpsimd.memset(scratch[:], 0.0)
+        nc.scalar.activation(scratch[:], scratch[:], TANH)
 
         identity = held.tile([P, P], BF16, name="identity")
         make_identity(nc, identity[:])
 
-        scratch = held.tile([P, 1], F32, name="scratch")
-        nc.vector.memset(scratch[:], 0.0)
-        nc.scalar.activation(scratch[:], scratch[:], TANH)
+        zeros = held.tile([P, BANK], BF16, name="zeros")
+        nc.vector.memset(zeros[:], 0.0)
+        idle_ps = psum.tile([P, BANK], F32, name="idle_ps", tag="bank7")
+        for i in range(WARM_UPS):
+            nc.tensor.matmul(idle_ps[:], zeros[:, 0:P], zeros[:], start=True, stop=True)
 
         table_t = held.tile([P, WORDS], BF16, name="table_t")
         for c in range(CHUNKS):
-            flipped = flip.tile([P, BLOCKS, P], BF16, name="flipped")
-            for b in range(BLOCKS):
-                nc.tensor.transpose(flipped[:, b, :], rows[c][:, b, :], identity[:])
-            columns = table_t[:, c * BLOCKS * P : (c + 1) * BLOCKS * P]
-            if c % 2 == 0:
-                nc.vector.tensor_copy(columns, flipped[:].rearrange("d b p -> d (b p)"))
+            columns = table_t[:, c * CHUNK : (c + 1) * CHUNK].rearrange("d (p a) -> d p a", a=RUN)
+            for half in range(2):
+                flipped = psum.tile([P, RUN // 2, P], BF16, name=f"flipped{c}_{half}", tag=f"bank{2 * c + half}")
+                for a in range(RUN // 2):
+                    nc.tensor.transpose(flipped[:, a, :], rows[c][:, half * (RUN // 2) + a, :], identity[:])
+                pairs = columns[:, :, half * (RUN // 2) : (half + 1) * (RUN // 2)]
+                in_order = flipped[:].rearrange("d a p -> d p a")
+                if half == 0:
+                    nc.vector.tensor_copy(pairs, in_order)
+                else:
+                    nc.scalar.copy(pairs, in_order)
+
+        h = []
+        for c in range(2):
+            h_ps = psum.tile([P, P], F32, name=f"h_ps{c}", tag=f"bank{c}")
+            piece = offsets[:, c * (P // 16) : (c + 1) * (P // 16)]
+            nc.tensor.matmul(h_ps[:], w_u_sb[:], table_t[:].indirect(piece), start=True, stop=True)
+            h.append(held.tile([P, P], BF16, name=f"h{c}"))
+            nc.scalar.activation(h[c][:], h_ps[:], TANH, bias=b_u_sb[:])
+        h_left, h_right = h
+
+        out_halves = out.rearrange("(c p r) q -> c p r q", c=2, r=ROWS)
+
+        def add_bias(r, sums_sb, sums_ps, bias_sb):
+            if r % 2 == 0:
+                nc.vector.tensor_scalar_add(sums_sb[:, r, :], sums_ps[:], bias_sb[:, r : r + 1])
             else:
-                nc.scalar.copy(columns, flipped[:].rearrange("d b p -> d (b p)"))
+                nc.scalar.activation(sums_sb[:, r, :], sums_ps[:], IDENTITY, bias=bias_sb[:, r : r + 1])
 
-        h_ps = psum.tile([P, LEAVES], F32, name="h_ps")
-        nc.tensor.matmul(h_ps[:], w_u_sb[:], table_t[:].indirect(offsets[:]), start=True, stop=True)
-        h = held.tile([P, LEAVES], BF16, name="h")
-        nc.scalar.activation(h[:], h_ps[:], TANH, bias=b_u_sb[:])
-        h_left, h_right = h[:, 0:P], h[:, P:LEAVES]
+        un_sb = held.tile([P, ROWS, P], F32, name="un_sb")
+        for r in range(ROWS):
+            un_ps = psum.tile([P, P], F32, name=f"un_ps{r}", tag=f"bank{2 + r}")
+            nc.tensor.matmul(un_ps[:], u_un_thirds[:, r, :], h_left[:], start=True, stop=True)
+            add_bias(r, un_sb, un_ps, b_un_sb)
+        nc.sync.dma_start(out_halves[1], un_sb[:])
 
-        un_ps = psum.tile([P, GATES, P], F32, name="un_ps")
-        bin_ps = psum.tile([P, GATES, P], F32, name="bin_ps")
-        for g in range(GATES):
-            gate = slice(g * P, (g + 1) * P)
-            nc.tensor.matmul(un_ps[:, g, :], u_un_sb[:, gate], h_left, start=True, stop=True)
-        for g in range(GATES):
-            gate = slice(g * P, (g + 1) * P)
-            nc.tensor.matmul(bin_ps[:, g, :], u_bin_sb[:, 0, gate], h_left, start=True, stop=False)
-            nc.tensor.matmul(bin_ps[:, g, :], u_bin_sb[:, 1, gate], h_right, start=False, stop=True)
-
-        out_blocks = out.rearrange("(c g p) q -> c p g q", c=2, p=P)
-        un_sb = held.tile([P, GATES, P], F32, name="un_sb")
-        nc.vector.tensor_tensor(un_sb[:], un_ps[:], b_un_sb[:].unsqueeze(2).to_broadcast([P, GATES, P]), ADD)
-        nc.sync.dma_start(out_blocks[1], un_sb[:])
-        bin_sb = held.tile([P, GATES, P], F32, name="bin_sb")
-        nc.vector.tensor_tensor(bin_sb[:], bin_ps[:], b_bin_sb[:].unsqueeze(2).to_broadcast([P, GATES, P]), ADD)
-        nc.sync.dma_start(out_blocks[0], bin_sb[:])
+        bin_sb = held.tile([P, ROWS, P], F32, name="bin_sb")
+        for r in range(ROWS):
+            bin_ps = psum.tile([P, P], F32, name=f"bin_ps{r}", tag=f"bank{5 + r}")
+            nc.tensor.matmul(bin_ps[:], u_bin_thirds[:, 0, r, :], h_left[:], start=True, stop=False)
+            nc.tensor.matmul(bin_ps[:], u_bin_thirds[:, 1, r, :], h_right[:], start=False, stop=True)
+            add_bias(r, bin_sb, bin_ps, b_bin_sb)
+        nc.sync.dma_start(out_halves[0], bin_sb[:])

@@ -64,17 +64,15 @@ def tile_mixedaritytreelstm_kernel(tc, table, w_u, b_u, u_bin, b_bin, u_un, b_un
 
         table_t = held.tile([P, WORDS], BF16, name="table_t")
         for c in range(CHUNKS):
+            flipped = psum.tile([P, RUN, P], BF16, name=f"flipped{c}", tag=f"bank{2 * c}")
+            for a in range(RUN):
+                nc.tensor.transpose(flipped[:, a, :], rows[c][:, a, :], identity[:])
             columns = table_t[:, c * CHUNK : (c + 1) * CHUNK].rearrange("d (p a) -> d p a", a=RUN)
-            for half in range(2):
-                flipped = psum.tile([P, RUN // 2, P], BF16, name=f"flipped{c}_{half}", tag=f"bank{2 * c + half}")
-                for a in range(RUN // 2):
-                    nc.tensor.transpose(flipped[:, a, :], rows[c][:, half * (RUN // 2) + a, :], identity[:])
-                pairs = columns[:, :, half * (RUN // 2) : (half + 1) * (RUN // 2)]
-                in_order = flipped[:].rearrange("d a p -> d p a")
-                if half == 0:
-                    nc.vector.tensor_copy(pairs, in_order)
-                else:
-                    nc.scalar.copy(pairs, in_order)
+            in_order = flipped[:].rearrange("d a p -> d p a")
+            if c % 2 == 0:
+                nc.vector.tensor_copy(columns, in_order)
+            else:
+                nc.scalar.copy(columns, in_order)
 
         h = []
         for c in range(2):

import concourse.mybir as mybir
from concourse.masks import make_identity

BF16, F32, U16 = mybir.dt.bfloat16, mybir.dt.float32, mybir.dt.uint16
TANH = mybir.ActivationFunctionType.Tanh
IDENTITY = mybir.ActivationFunctionType.Identity

P = 128
WORDS = 2048
LEAVES = 256
ROWS = 3
BANK = 512
CHUNKS = 4
CHUNK = WORDS // CHUNKS
RUN = CHUNK // P
WARM_UPS = 3

FLOPS = 2 * P * P * LEAVES + 2 * (2 * P) * (ROWS * P) * P + 2 * P * (ROWS * P) * P


def tile_mixedaritytreelstm_kernel(tc, table, w_u, b_u, u_bin, b_bin, u_un, b_un, offs, out):
    nc = tc.nc
    with (
        tc.tile_pool(name="held", bufs=1) as held,
        tc.psum_pool(name="psum", bufs=1) as psum,
    ):
        rows = []
        for c in range(CHUNKS):
            rows.append(held.tile([P, RUN, P], BF16, name=f"rows{c}"))
            nc.sync.dma_start(rows[c][:], table[c * CHUNK : (c + 1) * CHUNK, :].rearrange("(p a) d -> p a d", a=RUN))

        offsets = held.tile([P, LEAVES // 16], U16, name="offsets")
        nc.sync.dma_start(offsets[:], offs)

        w_u_sb = held.tile([P, P], BF16, name="w_u_sb")
        nc.sync.dma_start(w_u_sb[:], w_u)

        b_u_sb = held.tile([P, 1], F32, name="b_u_sb")
        nc.sync.dma_start(b_u_sb[:], b_u)
        u_un_sb = held.tile([P, ROWS * P], BF16, name="u_un_sb")
        nc.sync.dma_start(u_un_sb[:], u_un)
        u_bin_sb = held.tile([P, 2, ROWS * P], BF16, name="u_bin_sb")
        nc.sync.dma_start(u_bin_sb[:], u_bin.rearrange("(c k) m -> k c m", k=P))
        b_un_sb = held.tile([P, ROWS], F32, name="b_un_sb")
        nc.sync.dma_start(b_un_sb[:], b_un.rearrange("(p r) o -> p (r o)", r=ROWS))
        b_bin_sb = held.tile([P, ROWS], F32, name="b_bin_sb")
        nc.sync.dma_start(b_bin_sb[:], b_bin.rearrange("(p r) o -> p (r o)", r=ROWS))

        u_un_thirds = u_un_sb[:].rearrange("k (p r) -> k r p", r=ROWS)
        u_bin_thirds = u_bin_sb[:].rearrange("k c (p r) -> k c r p", r=ROWS)

        scratch = held.tile([P, 1], F32, name="scratch")
        nc.gpsimd.memset(scratch[:], 0.0)
        nc.scalar.activation(scratch[:], scratch[:], TANH)

        identity = held.tile([P, P], BF16, name="identity")
        make_identity(nc, identity[:])

        zeros = held.tile([P, BANK], BF16, name="zeros")
        nc.vector.memset(zeros[:], 0.0)
        idle_ps = psum.tile([P, BANK], F32, name="idle_ps", tag="bank7")
        for i in range(WARM_UPS):
            nc.tensor.matmul(idle_ps[:], zeros[:, 0:P], zeros[:], start=True, stop=True)

        table_t = held.tile([P, WORDS], BF16, name="table_t")
        for c in range(CHUNKS):
            flipped = psum.tile([P, RUN, P], BF16, name=f"flipped{c}", tag=f"bank{2 * c}")
            for a in range(RUN):
                nc.tensor.transpose(flipped[:, a, :], rows[c][:, a, :], identity[:])
            columns = table_t[:, c * CHUNK : (c + 1) * CHUNK].rearrange("d (p a) -> d p a", a=RUN)
            in_order = flipped[:].rearrange("d a p -> d p a")
            if c % 2 == 0:
                nc.vector.tensor_copy(columns, in_order)
            else:
                nc.scalar.copy(columns, in_order)

        h = []
        for c in range(2):
            h_ps = psum.tile([P, P], F32, name=f"h_ps{c}", tag=f"bank{c}")
            piece = offsets[:, c * (P // 16) : (c + 1) * (P // 16)]
            nc.tensor.matmul(h_ps[:], w_u_sb[:], table_t[:].indirect(piece), start=True, stop=True)
            h.append(held.tile([P, P], BF16, name=f"h{c}"))
            nc.scalar.activation(h[c][:], h_ps[:], TANH, bias=b_u_sb[:])
        h_left, h_right = h

        out_halves = out.rearrange("(c p r) q -> c p r q", c=2, r=ROWS)

        def add_bias(r, sums_sb, sums_ps, bias_sb):
            if r % 2 == 0:
                nc.vector.tensor_scalar_add(sums_sb[:, r, :], sums_ps[:], bias_sb[:, r : r + 1])
            else:
                nc.scalar.activation(sums_sb[:, r, :], sums_ps[:], IDENTITY, bias=bias_sb[:, r : r + 1])

        un_sb = held.tile([P, ROWS, P], F32, name="un_sb")
        for r in range(ROWS):
            un_ps = psum.tile([P, P], F32, name=f"un_ps{r}", tag=f"bank{2 + r}")
            nc.tensor.matmul(un_ps[:], u_un_thirds[:, r, :], h_left[:], start=True, stop=True)
            add_bias(r, un_sb, un_ps, b_un_sb)
        nc.sync.dma_start(out_halves[1], un_sb[:])

        bin_sb = held.tile([P, ROWS, P], F32, name="bin_sb")
        for r in range(ROWS):
            bin_ps = psum.tile([P, P], F32, name=f"bin_ps{r}", tag=f"bank{5 + r}")
            nc.tensor.matmul(bin_ps[:], u_bin_thirds[:, 0, r, :], h_left[:], start=True, stop=False)
            nc.tensor.matmul(bin_ps[:], u_bin_thirds[:, 1, r, :], h_right[:], start=False, stop=True)
            add_bias(r, bin_sb, bin_ps, b_bin_sb)
        nc.sync.dma_start(out_halves[0], bin_sb[:])
